import numpy as np
import ml_dtypes


def mxq(x, axis, fmt="e4m3"):
    dtype, down = {"e4m3": (ml_dtypes.float8_e4m3fn, 7), "e5m2": (ml_dtypes.float8_e5m2, 14)}[fmt]
    v = np.moveaxis(np.asarray(x, np.float32).astype(ml_dtypes.bfloat16).astype(np.float64), axis, -1)
    blocks = v.reshape(v.shape[:-1] + (-1, 32))
    amax = np.abs(blocks).max(-1, keepdims=True)
    byte = np.maximum(np.where(amax > 0, np.frexp(amax)[1] - 1 + 127, 0) - down, 1)
    scale = np.exp2(byte - 127.0)
    codes = (blocks / scale).astype(np.float32).astype(dtype).astype(np.float64)
    return np.moveaxis((codes * scale).reshape(v.shape), -1, axis)


WIDE = False


def mx_kscale(k):
    if not WIDE:
        return np.ones(k)
    levels = np.array([10, -10, 5, -5, 0])
    a = np.random.permutation(np.resize(levels, k // 512 * 4)).reshape(k // 512, 4)
    idx = np.arange(k)
    return np.exp2(a[idx // 512, idx % 128 // 32])


BF16 = ml_dtypes.bfloat16


def bf(x):
    return np.asarray(x, np.float32).astype(BF16)


def f64(x):
    return np.asarray(x).astype(np.float64)


B, GH, GW, F_IN, F_OUT = 2, 128, 64, 512, 128


def setup_inputs():
    s = mx_kscale(F_IN)
    return {"X": bf(np.random.standard_normal((B, GH * GW, F_IN)) * s),
            "W_gcn": bf(np.random.standard_normal((F_IN, F_OUT)) * 0.5 / np.sqrt(F_IN) / s[:, None]),
            "b": bf(np.random.standard_normal(F_OUT) * 0.3),
            "H": GH, "Wd": GW}


def _neighbor_sum(Xg):
    p = np.pad(Xg, ((0, 0), (1, 1), (1, 1), (0, 0)))
    return (p[:, :-2, 1:-1] + p[:, 2:, 1:-1]
            + p[:, 1:-1, :-2] + p[:, 1:-1, 2:])


def reference(X, W_gcn, b, H, Wd):
    X = f64(X)
    Bn, N, F = X.shape
    Xg = X.reshape(Bn, H, Wd, F)
    AX = _neighbor_sum(Xg).reshape(Bn, N, F)
    return (mxq(AX, 2, "e4m3") @ mxq(f64(W_gcn), 0, "e4m3")) + f64(b)

@@ -1,0 +1,155 @@
+from contextlib import ExitStack
+
+import concourse.mybir as mybir
+from concourse.masks import make_identity
+
+F32 = mybir.dt.float32
+BF16 = mybir.dt.bfloat16
+U32 = mybir.dt.uint32
+U8 = mybir.dt.uint8
+FP8X4 = mybir.dt.float8_e4m3fn_x4
+ADD = mybir.AluOpType.add
+
+P = 128
+NB, GH, GW, F_IN, F_OUT = 2, 128, 64, 512, 128
+FLOPS = 2 * NB * GH * GW * F_IN * F_OUT
+
+JC = 8
+NCH = GW // JC
+NS = 24
+XI = 132
+XS = XI * 4
+DS = 520
+
+
+def pieces(starts, n):
+    cuts = [0, n]
+    for st in starts:
+        k = NS - st % NS
+        while k < n:
+            cuts.append(k)
+            k += NS
+    cs = sorted(set(cuts))
+    return [(cs[i], cs[i + 1] - cs[i]) for i in range(len(cs) - 1)]
+
+
+def stream(bb, j):
+    return 1 + bb * (GW + 1) + j
+
+
+def tile_graphconvlayer_t_kernel(tc, X, W_gcn, b, H, Wd, out):
+    nc = tc.nc
+    assert H == GH and Wd == GW
+    xv = X.rearrange("b (i j) f -> b i (j f)", j=GW)
+    outv = out.rearrange("b (i j) o -> b i (j o)", j=GW)
+
+    with ExitStack() as ctx:
+        const = ctx.enter_context(tc.tile_pool(name="const", bufs=1))
+        xpool = ctx.enter_context(tc.tile_pool(name="xin", bufs=4))
+        gpool = ctx.enter_context(tc.tile_pool(name="grouped", bufs=2))
+        qpool = ctx.enter_context(tc.tile_pool(name="quant", bufs=2))
+        opool = ctx.enter_context(tc.tile_pool(name="outsb", bufs=3))
+        pst = ctx.enter_context(tc.psum_pool(name="pst", bufs=4))
+        pso = ctx.enter_context(tc.psum_pool(name="pso", bufs=2))
+
+        ident = const.tile([P, P], F32)
+        make_identity(nc, ident[:])
+
+        xtw = const.tile([P, NS * XI * 2], F32)
+        nc.vector.memset(xtw[:], 0.0)
+        xtw4 = xtw[:].rearrange("p (s i u) -> p s i u", i=XI, u=2)
+        xtb = xtw[:].bitcast(BF16).rearrange("p (s c) -> p s c", c=XS)
+        dr = const.tile([P, NS * DS], F32)
+        dv = dr[:].rearrange("p (s c) -> p s c", c=DS)
+
+        wraw = const.tile([P, 2, 2 * F_OUT], BF16)
+        nc.scalar.dma_start(out=wraw[:], in_=W_gcn.rearrange("(u p e) c -> p u (e c)", u=2, e=2))
+        wg = const.tile([P, 4 * F_OUT], BF16, align_bytes=64)
+        nc.vector.tensor_copy(
+            out=wg[:].rearrange("p (c u e) -> p c u e", u=2, e=2),
+            in_=wraw[:].rearrange("p u (e c) -> p c u e", e=2),
+        )
+        wc = const.tile([P, F_OUT], U32, align_bytes=64)
+        ws = const.tile([P, F_OUT], U8, align_bytes=64)
+        nc.vector.quantize_mx(out=wc[:].bitcast(FP8X4), scales=ws[:], in_=wg[:])
+
+        braw = const.tile([P, F_OUT], BF16)
+        nc.scalar.dma_start(out=braw[:], in_=b.partition_broadcast(P))
+        bias4 = const.tile([P, 4, F_OUT], F32)
+        for a in range(4):
+            nc.vector.tensor_copy(out=bias4[:, a, :], in_=braw[:])
+
+        def stage_a(bb, c):
+            xin = xpool.tile([P, JC * F_IN], BF16)
+            nc.sync.dma_start(out=xin[:], in_=xv[bb, :, c * JC * F_IN : (c + 1) * JC * F_IN])
+            xw = xin[:].bitcast(F32)
+            for pair in range(JC // 2):
+                bank = pst.tile([P, 4, P], F32)
+                for q in range(4):
+                    col = (pair * 4 + q) * P
+                    nc.tensor.transpose(out=bank[:, q, :], in_=xw[:, col : col + P], identity=ident[:])
+                s0 = stream(bb, c * JC + 2 * pair)
+                for off, n in pieces([s0], 2):
+                    r = (s0 + off) % NS
+                    nc.scalar.copy(
+                        out=xtw4[:, r : r + n, 1 : 1 + GH, :],
+                        in_=bank[:, 2 * off : 2 * (off + n), :].rearrange("p (j u) i -> p j i u", u=2),
+                    )
+
+        def stage_b(bb, c):
+            s0 = stream(bb, c * JC)
+            if c == NCH - 1:
+                z = (s0 + JC) % NS
+                nc.vector.memset(xtw4[:, z : z + 1, :, :], 0.0)
+            st = s0 - 1 if c == 0 else s0
+            cnt = JC + 1 if c == 0 else JC
+            for off, n in pieces([st, st + 1], cnt):
+                r = (st + off) % NS
+                r1 = (st + off + 1) % NS
+                nc.vector.tensor_tensor(
+                    out=dv[:, r : r + n, 0:516],
+                    in0=xtb[:, r : r + n, 0:516],
+                    in1=xtb[:, r1 : r1 + n, 4:520],
+                    op=ADD,
+                )
+            g = gpool.tile([P, JC, F_IN], BF16, align_bytes=64)
+            for off, n in pieces([s0, s0 - 1], JC):
+                r = (s0 + off) % NS
+                rm = (s0 + off - 1) % NS
+                nc.vector.tensor_tensor(
+                    out=g[:, off : off + n, :],
+                    in0=dv[:, r : r + n, 0:512],
+                    in1=dv[:, rm : rm + n, 4:516],
+                    op=ADD,
+                )
+            codes = qpool.tile([P, JC * P], U32, align_bytes=64)
+            scl = qpool.tile([P, JC * P], U8, align_bytes=64)
+            nc.vector.quantize_mx(
+                out=codes[:].bitcast(FP8X4), scales=scl[:], in_=g[:].rearrange("p j c -> p (j c)")
+            )
+            osb = opool.tile([P, JC, F_OUT], F32)
+            for h in range(JC // 4):
+                po = pso.tile([P, 4, F_OUT], F32)
+                for a in range(4):
+                    jl = h * 4 + a
+                    nc.tensor.matmul_mx(
+                        out=po[:, a, :],
+                        lhsT=codes[:, jl * P : (jl + 1) * P].bitcast(FP8X4),
+                        lhsT_scale=scl[:, jl * P : (jl + 1) * P],
+                        rhs=wc[:].bitcast(FP8X4),
+                        rhs_scale=ws[:],
+                        start=True,
+                        stop=True,
+                    )
+                nc.vector.tensor_tensor(out=osb[:, h * 4 : (h + 1) * 4, :], in0=po[:], in1=bias4[:], op=ADD)
+            nc.sync.dma_start(
+                out=outv[bb, :, c * JC * F_OUT : (c + 1) * JC * F_OUT],
+                in_=osb[:].rearrange("p j o -> p (j o)"),
+            )
+
+        chunks = [(bb, c) for bb in range(NB) for c in range(NCH)]
+        stage_a(*chunks[0])
+        for k in range(len(chunks)):
+            if k + 1 < len(chunks):
+                stage_a(*chunks[k + 1])
+            stage_b(*chunks[k])

@@ -20,6 +20,7 @@ NS = 24
 XI = 132
 XS = XI * 4
 DS = 520
+G_J = 4
 
 
 def pieces(starts, n):
@@ -46,10 +47,10 @@ def tile_graphconvlayer_t_kernel(tc, X, W_gcn, b, H, Wd, out):
     with ExitStack() as ctx:
         const = ctx.enter_context(tc.tile_pool(name="const", bufs=1))
         xpool = ctx.enter_context(tc.tile_pool(name="xin", bufs=4))
-        gpool = ctx.enter_context(tc.tile_pool(name="grouped", bufs=2))
+        gpool = ctx.enter_context(tc.tile_pool(name="grouped", bufs=3))
         qpool = ctx.enter_context(tc.tile_pool(name="quant", bufs=2))
         opool = ctx.enter_context(tc.tile_pool(name="outsb", bufs=3))
-        pst = ctx.enter_context(tc.psum_pool(name="pst", bufs=4))
+        pst = ctx.enter_context(tc.psum_pool(name="pst", bufs=6))
         pso = ctx.enter_context(tc.psum_pool(name="pso", bufs=2))
 
         ident = const.tile([P, P], F32)
@@ -79,49 +80,77 @@ def tile_graphconvlayer_t_kernel(tc, X, W_gcn, b, H, Wd, out):
         for a in range(4):
             nc.vector.tensor_copy(out=bias4[:, a, :], in_=braw[:])
 
-        def stage_a(bb, c):
-            xin = xpool.tile([P, JC * F_IN], BF16)
-            nc.sync.dma_start(out=xin[:], in_=xv[bb, :, c * JC * F_IN : (c + 1) * JC * F_IN])
-            xw = xin[:].bitcast(F32)
-            for pair in range(JC // 2):
-                bank = pst.tile([P, 4, P], F32)
-                for q in range(4):
-                    col = (pair * 4 + q) * P
-                    nc.tensor.transpose(out=bank[:, q, :], in_=xw[:, col : col + P], identity=ident[:])
-                s0 = stream(bb, c * JC + 2 * pair)
-                for off, n in pieces([s0], 2):
-                    r = (s0 + off) % NS
-                    nc.scalar.copy(
-                        out=xtw4[:, r : r + n, 1 : 1 + GH, :],
-                        in_=bank[:, 2 * off : 2 * (off + n), :].rearrange("p (j u) i -> p j i u", u=2),
-                    )
+        xin_of = {}
+        bank_of = {}
+        g_of = {}
 
-        def stage_b(bb, c):
-            s0 = stream(bb, c * JC)
-            if c == NCH - 1:
-                z = (s0 + JC) % NS
-                nc.vector.memset(xtw4[:, z : z + 1, :, :], 0.0)
-            st = s0 - 1 if c == 0 else s0
-            cnt = JC + 1 if c == 0 else JC
-            for off, n in pieces([st, st + 1], cnt):
-                r = (st + off) % NS
-                r1 = (st + off + 1) % NS
-                nc.vector.tensor_tensor(
-                    out=dv[:, r : r + n, 0:516],
-                    in0=xtb[:, r : r + n, 0:516],
-                    in1=xtb[:, r1 : r1 + n, 4:520],
-                    op=ADD,
-                )
-            g = gpool.tile([P, JC, F_IN], BF16, align_bytes=64)
-            for off, n in pieces([s0, s0 - 1], JC):
+        def emit_front(m):
+            bb, c, pair = m // (4 * NCH), (m // 4) % NCH, m % 4
+            if pair == 0:
+                xin = xpool.tile([P, JC * F_IN], BF16)
+                nc.sync.dma_start(out=xin[:], in_=xv[bb, :, c * JC * F_IN : (c + 1) * JC * F_IN])
+                xin_of[m // 4] = xin
+            xw = xin_of[m // 4][:].bitcast(F32)
+            bank = pst.tile([P, 4, P], F32)
+            for q in range(4):
+                col = (pair * 4 + q) * P
+                nc.tensor.transpose(out=bank[:, q, :], in_=xw[:, col : col + P], identity=ident[:])
+            s0 = stream(bb, c * JC + 2 * pair)
+            for off, n in pieces([s0], 2):
                 r = (s0 + off) % NS
-                rm = (s0 + off - 1) % NS
+                nc.scalar.copy(
+                    out=xtw4[:, r : r + n, 1 : 1 + GH, :],
+                    in_=bank[:, 2 * off : 2 * (off + n), :].rearrange("p (j u) i -> p j i u", u=2),
+                )
+            bank_of[m] = bank
+
+        def emit_pairsums(m):
+            bb, c, pair = m // (4 * NCH), (m // 4) % NCH, m % 4
+            s0 = stream(bb, c * JC + 2 * pair)
+            if c == NCH - 1 and pair == 3:
+                z = (s0 + 2) % NS
+                nc.vector.memset(xtw4[:, z : z + 1, :, :], 0.0)
+            if c == 0 and pair == 0:
+                r = (s0 - 1) % NS
+                nc.vector.tensor_copy(out=dv[:, r : r + 1, 4:520], in_=xtb[:, s0 % NS : s0 % NS + 1, 4:520])
+            bankb = bank_of[m][:].rearrange("p q i -> p (q i)").bitcast(BF16)
+            for off, n in pieces([s0, s0 + 1], 2):
+                r = (s0 + off) % NS
+                r1 = (s0 + off + 1) % NS
+                nc.scalar.copy(out=dv[:, r : r + n, 4:8], in_=xtb[:, r1 : r1 + n, 4:8])
+            for jl in range(2):
+                r = (s0 + jl) % NS
+                r1 = (s0 + jl + 1) % NS
                 nc.vector.tensor_tensor(
-                    out=g[:, off : off + n, :],
-                    in0=dv[:, r : r + n, 0:512],
-                    in1=dv[:, rm : rm + n, 4:516],
+                    out=dv[:, r, 8:520].rearrange("p (i u e) -> p i u e", u=2, e=2),
+                    in0=bankb[:, jl * 4 * P : (jl + 1) * 4 * P].rearrange("p (u i e) -> p i u e", u=2, e=2),
+                    in1=xtb[:, r1, 8:520].rearrange("p (i u e) -> p i u e", u=2, e=2),
                     op=ADD,
                 )
+
+        def second_add(eng, g, s0, lo, cnt):
+            for off, n in pieces([s0 + lo, s0 + lo - 1], cnt):
+                r = (s0 + lo + off) % NS
+                rm = (s0 + lo + off - 1) % NS
+                eng.tensor_tensor(
+                    out=g[:, lo + off : lo + off + n, :],
+                    in0=dv[:, r : r + n, 4:516],
+                    in1=dv[:, rm : rm + n, 8:520],
+                    op=ADD,
+                )
+
+        def emit_gpsimd_share(k, lo):
+            bb, c = k // NCH, k % NCH
+            if lo == 0:
+                g = gpool.tile([P, JC, F_IN], BF16, align_bytes=64)
+                g_of[k] = g
+            second_add(nc.gpsimd, g_of[k], stream(bb, c * JC), lo, 2)
+
+        def emit_back(k):
+            bb, c = k // NCH, k % NCH
+            s0 = stream(bb, c * JC)
+            g = g_of[k]
+            second_add(nc.vector, g, s0, G_J, JC - G_J)
             codes = qpool.tile([P, JC * P], U32, align_bytes=64)
             scl = qpool.tile([P, JC * P], U8, align_bytes=64)
             nc.vector.quantize_mx(
@@ -147,9 +176,13 @@ def tile_graphconvlayer_t_kernel(tc, X, W_gcn, b, H, Wd, out):
                 in_=osb[:].rearrange("p j o -> p (j o)"),
             )
 
-        chunks = [(bb, c) for bb in range(NB) for c in range(NCH)]
-        stage_a(*chunks[0])
-        for k in range(len(chunks)):
-            if k + 1 < len(chunks):
-                stage_a(*chunks[k + 1])
-            stage_b(*chunks[k])
+        n_banks = NB * NCH * 4
+        emit_front(0)
+        for m in range(n_banks):
+            if m + 1 < n_banks:
+                emit_front(m + 1)
+            emit_pairsums(m)
+            if 2 * (m % 4) < G_J:
+                emit_gpsimd_share(m // 4, 2 * (m % 4))
+            if m % 4 == 3:
+                emit_back(m // 4)

@@ -50,8 +50,10 @@ def tile_graphconvlayer_t_kernel(tc, X, W_gcn, b, H, Wd, out):
         gpool = ctx.enter_context(tc.tile_pool(name="grouped", bufs=3))
         qpool = ctx.enter_context(tc.tile_pool(name="quant", bufs=2))
         opool = ctx.enter_context(tc.tile_pool(name="outsb", bufs=3))
-        pst = ctx.enter_context(tc.psum_pool(name="pst", bufs=6))
+        pst = ctx.enter_context(tc.psum_pool(name="pst", bufs=4))
+        psy = ctx.enter_context(tc.psum_pool(name="psy", bufs=2))
         pso = ctx.enter_context(tc.psum_pool(name="pso", bufs=2))
+        ypool = ctx.enter_context(tc.tile_pool(name="ysb", bufs=3))
 
         ident = const.tile([P, P], F32)
         make_identity(nc, ident[:])
@@ -76,9 +78,14 @@ def tile_graphconvlayer_t_kernel(tc, X, W_gcn, b, H, Wd, out):
 
         braw = const.tile([P, F_OUT], BF16)
         nc.scalar.dma_start(out=braw[:], in_=b.partition_broadcast(P))
-        bias4 = const.tile([P, 4, F_OUT], F32)
-        for a in range(4):
-            nc.vector.tensor_copy(out=bias4[:, a, :], in_=braw[:])
+        bdiag = const.tile([P, F_OUT], F32)
+        nc.vector.tensor_tensor(out=bdiag[:], in0=braw[:], in1=ident[:], op=mybir.AluOpType.mult)
+        bcol = const.tile([P, 1], F32)
+        nc.vector.tensor_reduce(out=bcol[:], in_=bdiag[:], axis=mybir.AxisListType.X, op=ADD)
+        bias_t = const.tile([P, P], F32)
+        nc.vector.tensor_scalar(
+            out=bias_t[:], in0=ident[:], scalar1=0.0, scalar2=bcol[:, 0:1], op0=mybir.AluOpType.mult, op1=ADD
+        )
 
         xin_of = {}
         bank_of = {}
@@ -158,19 +165,32 @@ def tile_graphconvlayer_t_kernel(tc, X, W_gcn, b, H, Wd, out):
             )
             osb = opool.tile([P, JC, F_OUT], F32)
             for h in range(JC // 4):
+                py = psy.tile([P, 4 * P], F32)
+                nc.tensor.matmul_mx(
+                    out=py[:],
+                    lhsT=wc[:].bitcast(FP8X4),
+                    lhsT_scale=ws[:],
+                    rhs=codes[:, h * 4 * P : (h + 1) * 4 * P].bitcast(FP8X4),
+                    rhs_scale=scl[:, h * 4 * P : (h + 1) * 4 * P],
+                    start=True,
+                    stop=True,
+                )
+                ysb = ypool.tile([P, 4 * P], F32)
+                nc.scalar.copy(out=ysb[:], in_=py[:])
                 po = pso.tile([P, 4, F_OUT], F32)
                 for a in range(4):
-                    jl = h * 4 + a
-                    nc.tensor.matmul_mx(
+                    nc.tensor.matmul(
+                        out=po[:, a, :], lhsT=bias_t[:], rhs=ident[:], is_transpose=True, start=True, stop=False
+                    )
+                    nc.tensor.matmul(
                         out=po[:, a, :],
-                        lhsT=codes[:, jl * P : (jl + 1) * P].bitcast(FP8X4),
-                        lhsT_scale=scl[:, jl * P : (jl + 1) * P],
-                        rhs=wc[:].bitcast(FP8X4),
-                        rhs_scale=ws[:],
-                        start=True,
+                        lhsT=ysb[:, a * P : (a + 1) * P],
+                        rhs=ident[:],
+                        is_transpose=True,
+                        start=False,
                         stop=True,
                     )
-                nc.vector.tensor_tensor(out=osb[:, h * 4 : (h + 1) * 4, :], in0=po[:], in1=bias4[:], op=ADD)
+                nc.scalar.copy(out=osb[:, h * 4 : (h + 1) * 4, :], in_=po[:])
             nc.sync.dma_start(
                 out=outv[bb, :, c * JC * F_OUT : (c + 1) * JC * F_OUT],
                 in_=osb[:].rearrange("p j o -> p (j o)"),

@@ -9,6 +9,7 @@ U32 = mybir.dt.uint32
 U8 = mybir.dt.uint8
 FP8X4 = mybir.dt.float8_e4m3fn_x4
 ADD = mybir.AluOpType.add
+MULT = mybir.AluOpType.mult
 
 P = 128
 NB, GH, GW, F_IN, F_OUT = 2, 128, 64, 512, 128
@@ -16,26 +17,28 @@ FLOPS = 2 * NB * GH * GW * F_IN * F_OUT
 
 JC = 8
 NCH = GW // JC
-NS = 24
-XI = 132
-XS = XI * 4
+NT = F_IN // P
+NSO = 12
 DS = 520
-G_J = 4
-
-
-def pieces(starts, n):
-    cuts = [0, n]
-    for st in starts:
-        k = NS - st % NS
-        while k < n:
-            cuts.append(k)
-            k += NS
-    cs = sorted(set(cuts))
-    return [(cs[i], cs[i + 1] - cs[i]) for i in range(len(cs) - 1)]
+LAST = NB * (GW + 1)
 
 
 def stream(bb, j):
     return 1 + bb * (GW + 1) + j
+
+
+def column(s):
+    bb, r = s // (GW + 1), s % (GW + 1)
+    if r == 0:
+        return None
+    return (bb, r - 1)
+
+
+def pieces(start, n):
+    k = NSO - start % NSO
+    if k >= n:
+        return [(0, n)]
+    return [(0, k), (k, n - k)]
 
 
 def tile_graphconvlayer_t_kernel(tc, X, W_gcn, b, H, Wd, out):
@@ -46,118 +49,137 @@ def tile_graphconvlayer_t_kernel(tc, X, W_gcn, b, H, Wd, out):
 
     with ExitStack() as ctx:
         const = ctx.enter_context(tc.tile_pool(name="const", bufs=1))
-        xpool = ctx.enter_context(tc.tile_pool(name="xin", bufs=4))
+        xpool = ctx.enter_context(tc.tile_pool(name="xin", bufs=3))
+        fpool = ctx.enter_context(tc.tile_pool(name="xf", bufs=3))
         gpool = ctx.enter_context(tc.tile_pool(name="grouped", bufs=3))
         qpool = ctx.enter_context(tc.tile_pool(name="quant", bufs=2))
         opool = ctx.enter_context(tc.tile_pool(name="outsb", bufs=3))
-        pst = ctx.enter_context(tc.psum_pool(name="pst", bufs=4))
-        psy = ctx.enter_context(tc.psum_pool(name="psy", bufs=2))
+        psd = ctx.enter_context(tc.psum_pool(name="psd", bufs=6))
         pso = ctx.enter_context(tc.psum_pool(name="pso", bufs=2))
-        ypool = ctx.enter_context(tc.tile_pool(name="ysb", bufs=3))
 
         ident = const.tile([P, P], F32)
         make_identity(nc, ident[:])
+        sh_up = const.tile([P, P], F32)
+        nc.vector.memset(sh_up[:], 0.0)
+        nc.vector.tensor_copy(out=sh_up[:, 1:P], in_=ident[:, 0 : P - 1])
+        sh_dn = const.tile([P, P], F32)
+        nc.vector.memset(sh_dn[:], 0.0)
+        nc.vector.tensor_copy(out=sh_dn[:, 0 : P - 1], in_=ident[:, 1:P])
 
-        xtw = const.tile([P, NS * XI * 2], F32)
-        nc.vector.memset(xtw[:], 0.0)
-        xtw4 = xtw[:].rearrange("p (s i u) -> p s i u", i=XI, u=2)
-        xtb = xtw[:].bitcast(BF16).rearrange("p (s c) -> p s c", c=XS)
-        dr = const.tile([P, NS * DS], F32)
-        dv = dr[:].rearrange("p (s c) -> p s c", c=DS)
+        xin_of = {}
+        xf_of = {}
 
-        wraw = const.tile([P, 2, 2 * F_OUT], BF16)
-        nc.scalar.dma_start(out=wraw[:], in_=W_gcn.rearrange("(u p e) c -> p u (e c)", u=2, e=2))
-        wg = const.tile([P, 4 * F_OUT], BF16, align_bytes=64)
-        nc.vector.tensor_copy(
-            out=wg[:].rearrange("p (c u e) -> p c u e", u=2, e=2),
-            in_=wraw[:].rearrange("p u (e c) -> p c u e", e=2),
-        )
+        def emit_load_cast(k):
+            bb, c = k // NCH, k % NCH
+            xin = xpool.tile([P, JC * F_IN], BF16)
+            xf = fpool.tile([P, JC * F_IN], F32)
+            n_dma = 4 if k == 0 else 1
+            w = JC * F_IN // n_dma
+            for d in range(n_dma):
+                nc.sync.dma_start(
+                    out=xin[:, d * w : (d + 1) * w], in_=xv[bb, :, c * JC * F_IN + d * w : c * JC * F_IN + (d + 1) * w]
+                )
+            for q in range(4):
+                lo, hi = q * 2 * F_IN, (q + 1) * 2 * F_IN
+                if q % 2 == 0:
+                    nc.scalar.copy(out=xf[:, lo:hi], in_=xin[:, lo:hi])
+                else:
+                    nc.gpsimd.tensor_scalar(
+                        out=xf[:, lo:hi], in0=xin[:, lo:hi], scalar1=1.0, scalar2=0.0, op0=MULT, op1=ADD
+                    )
+            xin_of[k] = xin
+            xf_of[k] = xf
+
+        emit_load_cast(0)
+
+        wraw = const.tile([P, NT, F_OUT], BF16)
+        nc.scalar.dma_start(out=wraw[:], in_=W_gcn.rearrange("(t p) c -> p t c", p=P))
+        wg = const.tile([P, F_OUT, NT], BF16, align_bytes=64)
+        nc.vector.tensor_copy(out=wg[:], in_=wraw[:].rearrange("p t c -> p c t"))
         wc = const.tile([P, F_OUT], U32, align_bytes=64)
         ws = const.tile([P, F_OUT], U8, align_bytes=64)
-        nc.vector.quantize_mx(out=wc[:].bitcast(FP8X4), scales=ws[:], in_=wg[:])
+        nc.vector.quantize_mx(out=wc[:].bitcast(FP8X4), scales=ws[:], in_=wg[:].rearrange("p c t -> p (c t)"))
 
         braw = const.tile([P, F_OUT], BF16)
         nc.scalar.dma_start(out=braw[:], in_=b.partition_broadcast(P))
-        bdiag = const.tile([P, F_OUT], F32)
-        nc.vector.tensor_tensor(out=bdiag[:], in0=braw[:], in1=ident[:], op=mybir.AluOpType.mult)
-        bcol = const.tile([P, 1], F32)
-        nc.vector.tensor_reduce(out=bcol[:], in_=bdiag[:], axis=mybir.AxisListType.X, op=ADD)
-        bias_t = const.tile([P, P], F32)
-        nc.vector.tensor_scalar(
-            out=bias_t[:], in0=ident[:], scalar1=0.0, scalar2=bcol[:, 0:1], op0=mybir.AluOpType.mult, op1=ADD
-        )
+        bias4 = const.tile([P, 4, F_OUT], F32)
+        for a in range(4):
+            nc.vector.tensor_copy(out=bias4[:, a, :], in_=braw[:])
 
-        xin_of = {}
+        edge = []
+        for e in range(2):
+            xe = const.tile([P, F_IN], BF16, name="xe%d" % e)
+            row0 = e * (GH - 1) * GW
+            for bb in range(NB):
+                nc.scalar.dma_start(out=xe[bb * GW : (bb + 1) * GW, :], in_=X[bb, row0 : row0 + GW, :])
+            xef = const.tile([P, F_IN], F32, name="xef%d" % e)
+            nc.vector.tensor_copy(out=xef[:], in_=xe[:])
+            pe = psd.tile([P, NT, P], F32, tag="bank")
+            for t in range(NT):
+                nc.tensor.transpose(out=pe[:, t, :], in_=xef[:, t * P : (t + 1) * P], identity=ident[:])
+            ed = const.tile([P, LAST + 1, NT], F32, name="edge%d" % e)
+            nc.vector.memset(ed[:], 0.0)
+            for bb in range(NB):
+                nc.vector.tensor_copy(
+                    out=ed[:, stream(bb, 0) : stream(bb, 0) + GW, :],
+                    in_=pe[:, :, bb * GW : (bb + 1) * GW].rearrange("p t n -> p n t"),
+                )
+            edge.append(ed)
+
+        dsb = const.tile([P, NSO, DS], F32)
         bank_of = {}
-        g_of = {}
 
-        def emit_front(m):
-            bb, c, pair = m // (4 * NCH), (m // 4) % NCH, m % 4
-            if pair == 0:
-                xin = xpool.tile([P, JC * F_IN], BF16)
-                nc.sync.dma_start(out=xin[:], in_=xv[bb, :, c * JC * F_IN : (c + 1) * JC * F_IN])
-                xin_of[m // 4] = xin
-            xw = xin_of[m // 4][:].bitcast(F32)
-            bank = pst.tile([P, 4, P], F32)
-            for q in range(4):
-                col = (pair * 4 + q) * P
-                nc.tensor.transpose(out=bank[:, q, :], in_=xw[:, col : col + P], identity=ident[:])
-            s0 = stream(bb, c * JC + 2 * pair)
-            for off, n in pieces([s0], 2):
-                r = (s0 + off) % NS
+        def block(col, t):
+            bb, j = col
+            k, jl = bb * NCH + j // JC, j % JC
+            return xf_of[k][:, jl * F_IN + t * P : jl * F_IN + (t + 1) * P]
+
+        def emit_pairsum(s):
+            here, right = column(s), column(s + 1)
+            if s % 2 == 0:
+                terms = [(here, sh_up), (right, ident)]
+            else:
+                terms = [(right, sh_dn), (here, ident)]
+            terms = [(col, perm) for col, perm in terms if col is not None]
+            bank = psd.tile([P, NT, P], F32, tag="bank")
+            for t in range(NT):
+                for n, (col, perm) in enumerate(terms):
+                    nc.tensor.matmul(
+                        out=bank[:, t, :],
+                        lhsT=block(col, t),
+                        rhs=perm[:],
+                        is_transpose=True,
+                        start=(n == 0),
+                        stop=(n == len(terms) - 1),
+                    )
+            if s % 2 == 0:
+                bank_of[s] = bank
+            else:
+                r = (s // 2) % NSO
                 nc.scalar.copy(
-                    out=xtw4[:, r : r + n, 1 : 1 + GH, :],
-                    in_=bank[:, 2 * off : 2 * (off + n), :].rearrange("p (j u) i -> p j i u", u=2),
+                    out=dsb[:, r, 4:516].rearrange("p (a t) -> p a t", t=NT), in_=bank[:].rearrange("p t a -> p a t")
                 )
-            bank_of[m] = bank
 
-        def emit_pairsums(m):
-            bb, c, pair = m // (4 * NCH), (m // 4) % NCH, m % 4
-            s0 = stream(bb, c * JC + 2 * pair)
-            if c == NCH - 1 and pair == 3:
-                z = (s0 + 2) % NS
-                nc.vector.memset(xtw4[:, z : z + 1, :, :], 0.0)
-            if c == 0 and pair == 0:
-                r = (s0 - 1) % NS
-                nc.vector.tensor_copy(out=dv[:, r : r + 1, 4:520], in_=xtb[:, s0 % NS : s0 % NS + 1, 4:520])
-            bankb = bank_of[m][:].rearrange("p q i -> p (q i)").bitcast(BF16)
-            for off, n in pieces([s0, s0 + 1], 2):
-                r = (s0 + off) % NS
-                r1 = (s0 + off + 1) % NS
-                nc.scalar.copy(out=dv[:, r : r + n, 4:8], in_=xtb[:, r1 : r1 + n, 4:8])
-            for jl in range(2):
-                r = (s0 + jl) % NS
-                r1 = (s0 + jl + 1) % NS
+        def emit_second_add(s, g, jl):
+            if s % 2 == 0:
+                r = ((s - 1) // 2) % NSO
                 nc.vector.tensor_tensor(
-                    out=dv[:, r, 8:520].rearrange("p (i u e) -> p i u e", u=2, e=2),
-                    in0=bankb[:, jl * 4 * P : (jl + 1) * 4 * P].rearrange("p (u i e) -> p i u e", u=2, e=2),
-                    in1=xtb[:, r1, 8:520].rearrange("p (i u e) -> p i u e", u=2, e=2),
+                    out=g[:, jl, :].rearrange("p (i t) -> p i t", t=NT),
+                    in0=bank_of[s][:].rearrange("p t i -> p i t"),
+                    in1=dsb[:, r, 4:516].rearrange("p (i t) -> p i t", t=NT),
+                    op=ADD,
+                )
+            else:
+                r = (s // 2) % NSO
+                nc.vector.tensor_tensor(
+                    out=g[:, jl, 0:508].rearrange("p (i t) -> p i t", t=NT),
+                    in0=bank_of[s - 1][:, :, 1:P].rearrange("p t i -> p i t"),
+                    in1=dsb[:, r, 0:508].rearrange("p (i t) -> p i t", t=NT),
                     op=ADD,
                 )
 
-        def second_add(eng, g, s0, lo, cnt):
-            for off, n in pieces([s0 + lo, s0 + lo - 1], cnt):
-                r = (s0 + lo + off) % NS
-                rm = (s0 + lo + off - 1) % NS
-                eng.tensor_tensor(
-                    out=g[:, lo + off : lo + off + n, :],
-                    in0=dv[:, r : r + n, 4:516],
-                    in1=dv[:, rm : rm + n, 8:520],
-                    op=ADD,
-                )
-
-        def emit_gpsimd_share(k, lo):
+        def emit_back(k, g):
             bb, c = k // NCH, k % NCH
-            if lo == 0:
-                g = gpool.tile([P, JC, F_IN], BF16, align_bytes=64)
-                g_of[k] = g
-            second_add(nc.gpsimd, g_of[k], stream(bb, c * JC), lo, 2)
-
-        def emit_back(k):
-            bb, c = k // NCH, k % NCH
-            s0 = stream(bb, c * JC)
-            g = g_of[k]
-            second_add(nc.vector, g, s0, G_J, JC - G_J)
             codes = qpool.tile([P, JC * P], U32, align_bytes=64)
             scl = qpool.tile([P, JC * P], U8, align_bytes=64)
             nc.vector.quantize_mx(
@@ -165,44 +187,49 @@ def tile_graphconvlayer_t_kernel(tc, X, W_gcn, b, H, Wd, out):
             )
             osb = opool.tile([P, JC, F_OUT], F32)
             for h in range(JC // 4):
-                py = psy.tile([P, 4 * P], F32)
-                nc.tensor.matmul_mx(
-                    out=py[:],
-                    lhsT=wc[:].bitcast(FP8X4),
-                    lhsT_scale=ws[:],
-                    rhs=codes[:, h * 4 * P : (h + 1) * 4 * P].bitcast(FP8X4),
-                    rhs_scale=scl[:, h * 4 * P : (h + 1) * 4 * P],
-                    start=True,
-                    stop=True,
-                )
-                ysb = ypool.tile([P, 4 * P], F32)
-                nc.scalar.copy(out=ysb[:], in_=py[:])
                 po = pso.tile([P, 4, F_OUT], F32)
                 for a in range(4):
-                    nc.tensor.matmul(
-                        out=po[:, a, :], lhsT=bias_t[:], rhs=ident[:], is_transpose=True, start=True, stop=False
-                    )
-                    nc.tensor.matmul(
+                    jl = h * 4 + a
+                    nc.tensor.matmul_mx(
                         out=po[:, a, :],
-                        lhsT=ysb[:, a * P : (a + 1) * P],
-                        rhs=ident[:],
-                        is_transpose=True,
-                        start=False,
+                        lhsT=codes[:, jl * P : (jl + 1) * P].bitcast(FP8X4),
+                        lhsT_scale=scl[:, jl * P : (jl + 1) * P],
+                        rhs=wc[:].bitcast(FP8X4),
+                        rhs_scale=ws[:],
+                        start=True,
                         stop=True,
                     )
-                nc.scalar.copy(out=osb[:, h * 4 : (h + 1) * 4, :], in_=po[:])
+                nc.vector.tensor_tensor(out=osb[:, h * 4 : (h + 1) * 4, :], in0=po[:], in1=bias4[:], op=ADD)
             nc.sync.dma_start(
                 out=outv[bb, :, c * JC * F_OUT : (c + 1) * JC * F_OUT],
                 in_=osb[:].rearrange("p j o -> p (j o)"),
             )
 
-        n_banks = NB * NCH * 4
-        emit_front(0)
-        for m in range(n_banks):
-            if m + 1 < n_banks:
-                emit_front(m + 1)
-            emit_pairsums(m)
-            if 2 * (m % 4) < G_J:
-                emit_gpsimd_share(m // 4, 2 * (m % 4))
-            if m % 4 == 3:
-                emit_back(m // 4)
+        n_chunks = NB * NCH
+        for k in range(n_chunks):
+            bb, c = k // NCH, k % NCH
+            if k + 1 < n_chunks:
+                emit_load_cast(k + 1)
+            s0 = stream(bb, c * JC)
+            if c == 0:
+                emit_pairsum(s0 - 1)
+            first_odd = s0 + (1 - s0 % 2)
+            for off, n in pieces(first_odd // 2, JC // 2):
+                r = (first_odd // 2 + off) % NSO
+                lo = first_odd + 1 + 2 * off
+                nc.scalar.copy(out=dsb[:, r : r + n, 0:4], in_=edge[0][:, lo : lo + 2 * n - 1 : 2, :])
+            g = gpool.tile([P, JC, F_IN], BF16, align_bytes=64)
+            for jl in range(JC):
+                emit_pairsum(s0 + jl)
+                emit_second_add(s0 + jl, g, jl)
+            for off, n in pieces(first_odd // 2, JC // 2):
+                r = (first_odd // 2 + off) % NSO
+                lo = first_odd - 1 + 2 * off
+                j0 = first_odd - s0 + 2 * off
+                nc.vector.tensor_tensor(
+                    out=g[:, j0 : j0 + 2 * n - 1 : 2, 508:512],
+                    in0=dsb[:, r : r + n, 508:512],
+                    in1=edge[1][:, lo : lo + 2 * n - 1 : 2, :],
+                    op=ADD,
+                )
+            emit_back(k, g)

@@ -9,7 +9,6 @@ U32 = mybir.dt.uint32
 U8 = mybir.dt.uint8
 FP8X4 = mybir.dt.float8_e4m3fn_x4
 ADD = mybir.AluOpType.add
-MULT = mybir.AluOpType.mult
 
 P = 128
 NB, GH, GW, F_IN, F_OUT = 2, 128, 64, 512, 128
@@ -17,28 +16,26 @@ FLOPS = 2 * NB * GH * GW * F_IN * F_OUT
 
 JC = 8
 NCH = GW // JC
-NT = F_IN // P
-NSO = 12
+NS = 24
+XI = 132
+XS = XI * 4
 DS = 520
-LAST = NB * (GW + 1)
+G_J = 3
+
+
+def pieces(starts, n):
+    cuts = [0, n]
+    for st in starts:
+        k = NS - st % NS
+        while k < n:
+            cuts.append(k)
+            k += NS
+    cs = sorted(set(cuts))
+    return [(cs[i], cs[i + 1] - cs[i]) for i in range(len(cs) - 1)]
 
 
 def stream(bb, j):
     return 1 + bb * (GW + 1) + j
-
-
-def column(s):
-    bb, r = s // (GW + 1), s % (GW + 1)
-    if r == 0:
-        return None
-    return (bb, r - 1)
-
-
-def pieces(start, n):
-    k = NSO - start % NSO
-    if k >= n:
-        return [(0, n)]
-    return [(0, k), (k, n - k)]
 
 
 def tile_graphconvlayer_t_kernel(tc, X, W_gcn, b, H, Wd, out):
@@ -49,137 +46,122 @@ def tile_graphconvlayer_t_kernel(tc, X, W_gcn, b, H, Wd, out):
 
     with ExitStack() as ctx:
         const = ctx.enter_context(tc.tile_pool(name="const", bufs=1))
-        xpool = ctx.enter_context(tc.tile_pool(name="xin", bufs=3))
-        fpool = ctx.enter_context(tc.tile_pool(name="xf", bufs=3))
+        xpool = ctx.enter_context(tc.tile_pool(name="xin", bufs=4))
         gpool = ctx.enter_context(tc.tile_pool(name="grouped", bufs=3))
         qpool = ctx.enter_context(tc.tile_pool(name="quant", bufs=2))
         opool = ctx.enter_context(tc.tile_pool(name="outsb", bufs=3))
-        psd = ctx.enter_context(tc.psum_pool(name="psd", bufs=6))
+        pst = ctx.enter_context(tc.psum_pool(name="pst", bufs=4))
+        psy = ctx.enter_context(tc.psum_pool(name="psy", bufs=2))
         pso = ctx.enter_context(tc.psum_pool(name="pso", bufs=2))
+        ypool = ctx.enter_context(tc.tile_pool(name="ysb", bufs=3))
 
         ident = const.tile([P, P], F32)
         make_identity(nc, ident[:])
-        sh_up = const.tile([P, P], F32)
-        nc.vector.memset(sh_up[:], 0.0)
-        nc.vector.tensor_copy(out=sh_up[:, 1:P], in_=ident[:, 0 : P - 1])
-        sh_dn = const.tile([P, P], F32)
-        nc.vector.memset(sh_dn[:], 0.0)
-        nc.vector.tensor_copy(out=sh_dn[:, 0 : P - 1], in_=ident[:, 1:P])
 
-        xin_of = {}
-        xf_of = {}
+        xtw = const.tile([P, NS * XI * 2], F32)
+        nc.vector.memset(xtw[:], 0.0)
+        xtw4 = xtw[:].rearrange("p (s i u) -> p s i u", i=XI, u=2)
+        xtb = xtw[:].bitcast(BF16).rearrange("p (s c) -> p s c", c=XS)
+        dr = const.tile([P, NS * DS], F32)
+        dv = dr[:].rearrange("p (s c) -> p s c", c=DS)
 
-        def emit_load_cast(k):
-            bb, c = k // NCH, k % NCH
-            xin = xpool.tile([P, JC * F_IN], BF16)
-            xf = fpool.tile([P, JC * F_IN], F32)
-            n_dma = 4 if k == 0 else 1
-            w = JC * F_IN // n_dma
-            for d in range(n_dma):
-                nc.sync.dma_start(
-                    out=xin[:, d * w : (d + 1) * w], in_=xv[bb, :, c * JC * F_IN + d * w : c * JC * F_IN + (d + 1) * w]
-                )
-            for q in range(4):
-                lo, hi = q * 2 * F_IN, (q + 1) * 2 * F_IN
-                if q % 2 == 0:
-                    nc.scalar.copy(out=xf[:, lo:hi], in_=xin[:, lo:hi])
-                else:
-                    nc.gpsimd.tensor_scalar(
-                        out=xf[:, lo:hi], in0=xin[:, lo:hi], scalar1=1.0, scalar2=0.0, op0=MULT, op1=ADD
-                    )
-            xin_of[k] = xin
-            xf_of[k] = xf
-
-        emit_load_cast(0)
-
-        wraw = const.tile([P, NT, F_OUT], BF16)
-        nc.scalar.dma_start(out=wraw[:], in_=W_gcn.rearrange("(t p) c -> p t c", p=P))
-        wg = const.tile([P, F_OUT, NT], BF16, align_bytes=64)
-        nc.vector.tensor_copy(out=wg[:], in_=wraw[:].rearrange("p t c -> p c t"))
+        wraw = const.tile([P, 2, 2 * F_OUT], BF16)
+        nc.scalar.dma_start(out=wraw[:], in_=W_gcn.rearrange("(u p e) c -> p u (e c)", u=2, e=2))
+        wg = const.tile([P, 4 * F_OUT], BF16, align_bytes=64)
+        nc.vector.tensor_copy(
+            out=wg[:].rearrange("p (c u e) -> p c u e", u=2, e=2),
+            in_=wraw[:].rearrange("p u (e c) -> p c u e", e=2),
+        )
         wc = const.tile([P, F_OUT], U32, align_bytes=64)
         ws = const.tile([P, F_OUT], U8, align_bytes=64)
-        nc.vector.quantize_mx(out=wc[:].bitcast(FP8X4), scales=ws[:], in_=wg[:].rearrange("p c t -> p (c t)"))
+        nc.vector.quantize_mx(out=wc[:].bitcast(FP8X4), scales=ws[:], in_=wg[:])
 
         braw = const.tile([P, F_OUT], BF16)
         nc.scalar.dma_start(out=braw[:], in_=b.partition_broadcast(P))
-        bias4 = const.tile([P, 4, F_OUT], F32)
-        for a in range(4):
-            nc.vector.tensor_copy(out=bias4[:, a, :], in_=braw[:])
+        bdiag = const.tile([P, F_OUT], F32)
+        nc.vector.tensor_tensor(out=bdiag[:], in0=braw[:], in1=ident[:], op=mybir.AluOpType.mult)
+        bcol = const.tile([P, 1], F32)
+        nc.vector.tensor_reduce(out=bcol[:], in_=bdiag[:], axis=mybir.AxisListType.X, op=ADD)
+        bias_t = const.tile([P, P], F32)
+        nc.vector.tensor_scalar(
+            out=bias_t[:], in0=ident[:], scalar1=0.0, scalar2=bcol[:, 0:1], op0=mybir.AluOpType.mult, op1=ADD
+        )
 
-        edge = []
-        for e in range(2):
-            xe = const.tile([P, F_IN], BF16, name="xe%d" % e)
-            row0 = e * (GH - 1) * GW
-            for bb in range(NB):
-                nc.scalar.dma_start(out=xe[bb * GW : (bb + 1) * GW, :], in_=X[bb, row0 : row0 + GW, :])
-            xef = const.tile([P, F_IN], F32, name="xef%d" % e)
-            nc.vector.tensor_copy(out=xef[:], in_=xe[:])
-            pe = psd.tile([P, NT, P], F32, tag="bank")
-            for t in range(NT):
-                nc.tensor.transpose(out=pe[:, t, :], in_=xef[:, t * P : (t + 1) * P], identity=ident[:])
-            ed = const.tile([P, LAST + 1, NT], F32, name="edge%d" % e)
-            nc.vector.memset(ed[:], 0.0)
-            for bb in range(NB):
-                nc.vector.tensor_copy(
-                    out=ed[:, stream(bb, 0) : stream(bb, 0) + GW, :],
-                    in_=pe[:, :, bb * GW : (bb + 1) * GW].rearrange("p t n -> p n t"),
-                )
-            edge.append(ed)
-
-        dsb = const.tile([P, NSO, DS], F32)
+        xin_of = {}
         bank_of = {}
+        g_of = {}
 
-        def block(col, t):
-            bb, j = col
-            k, jl = bb * NCH + j // JC, j % JC
-            return xf_of[k][:, jl * F_IN + t * P : jl * F_IN + (t + 1) * P]
-
-        def emit_pairsum(s):
-            here, right = column(s), column(s + 1)
-            if s % 2 == 0:
-                terms = [(here, sh_up), (right, ident)]
-            else:
-                terms = [(right, sh_dn), (here, ident)]
-            terms = [(col, perm) for col, perm in terms if col is not None]
-            bank = psd.tile([P, NT, P], F32, tag="bank")
-            for t in range(NT):
-                for n, (col, perm) in enumerate(terms):
-                    nc.tensor.matmul(
-                        out=bank[:, t, :],
-                        lhsT=block(col, t),
-                        rhs=perm[:],
-                        is_transpose=True,
-                        start=(n == 0),
-                        stop=(n == len(terms) - 1),
-                    )
-            if s % 2 == 0:
-                bank_of[s] = bank
-            else:
-                r = (s // 2) % NSO
+        def emit_front(m):
+            bb, c, pair = m // (4 * NCH), (m // 4) % NCH, m % 4
+            if pair == 0:
+                xin = xpool.tile([P, JC * F_IN], BF16)
+                n_dma = 4 if m == 0 else 1
+                w = JC * F_IN // n_dma
+                for d in range(n_dma):
+                    lo = c * JC * F_IN + d * w
+                    nc.sync.dma_start(out=xin[:, d * w : (d + 1) * w], in_=xv[bb, :, lo : lo + w])
+                xin_of[m // 4] = xin
+            xw = xin_of[m // 4][:].bitcast(F32)
+            bank = pst.tile([P, 4, P], F32)
+            for q in range(4):
+                col = (pair * 4 + q) * P
+                nc.tensor.transpose(out=bank[:, q, :], in_=xw[:, col : col + P], identity=ident[:])
+            s0 = stream(bb, c * JC + 2 * pair)
+            for off, n in pieces([s0], 2):
+                r = (s0 + off) % NS
                 nc.scalar.copy(
-                    out=dsb[:, r, 4:516].rearrange("p (a t) -> p a t", t=NT), in_=bank[:].rearrange("p t a -> p a t")
+                    out=xtw4[:, r : r + n, 1 : 1 + GH, :],
+                    in_=bank[:, 2 * off : 2 * (off + n), :].rearrange("p (j u) i -> p j i u", u=2),
                 )
+            bank_of[m] = bank
 
-        def emit_second_add(s, g, jl):
-            if s % 2 == 0:
-                r = ((s - 1) // 2) % NSO
+        def emit_pairsums(m):
+            bb, c, pair = m // (4 * NCH), (m // 4) % NCH, m % 4
+            s0 = stream(bb, c * JC + 2 * pair)
+            if c == NCH - 1 and pair == 3:
+                z = (s0 + 2) % NS
+                nc.vector.memset(xtw4[:, z : z + 1, :, :], 0.0)
+            if c == 0 and pair == 0:
+                r = (s0 - 1) % NS
+                nc.vector.tensor_copy(out=dv[:, r : r + 1, 4:520], in_=xtb[:, s0 % NS : s0 % NS + 1, 4:520])
+            bankb = bank_of[m][:].rearrange("p q i -> p (q i)").bitcast(BF16)
+            for off, n in pieces([s0, s0 + 1], 2):
+                r = (s0 + off) % NS
+                r1 = (s0 + off + 1) % NS
+                nc.scalar.copy(out=dv[:, r : r + n, 4:8], in_=xtb[:, r1 : r1 + n, 4:8])
+            for jl in range(2):
+                r = (s0 + jl) % NS
+                r1 = (s0 + jl + 1) % NS
                 nc.vector.tensor_tensor(
-                    out=g[:, jl, :].rearrange("p (i t) -> p i t", t=NT),
-                    in0=bank_of[s][:].rearrange("p t i -> p i t"),
-                    in1=dsb[:, r, 4:516].rearrange("p (i t) -> p i t", t=NT),
+                    out=dv[:, r, 8:520].rearrange("p (i u e) -> p i u e", u=2, e=2),
+                    in0=bankb[:, jl * 4 * P : (jl + 1) * 4 * P].rearrange("p (u i e) -> p i u e", u=2, e=2),
+                    in1=xtb[:, r1, 8:520].rearrange("p (i u e) -> p i u e", u=2, e=2),
                     op=ADD,
                 )
-            else:
-                r = (s // 2) % NSO
-                nc.vector.tensor_tensor(
-                    out=g[:, jl, 0:508].rearrange("p (i t) -> p i t", t=NT),
-                    in0=bank_of[s - 1][:, :, 1:P].rearrange("p t i -> p i t"),
-                    in1=dsb[:, r, 0:508].rearrange("p (i t) -> p i t", t=NT),
+
+        def second_add(eng, g, s0, lo, cnt):
+            for off, n in pieces([s0 + lo, s0 + lo - 1], cnt):
+                r = (s0 + lo + off) % NS
+                rm = (s0 + lo + off - 1) % NS
+                eng.tensor_tensor(
+                    out=g[:, lo + off : lo + off + n, :],
+                    in0=dv[:, r : r + n, 4:516],
+                    in1=dv[:, rm : rm + n, 8:520],
                     op=ADD,
                 )
 
-        def emit_back(k, g):
+        def emit_gpsimd_share(k, lo):
             bb, c = k // NCH, k % NCH
+            if lo == 0:
+                g = gpool.tile([P, JC, F_IN], BF16, align_bytes=64)
+                g_of[k] = g
+            second_add(nc.gpsimd, g_of[k], stream(bb, c * JC), lo, min(2, G_J - lo))
+
+        def emit_back(k):
+            bb, c = k // NCH, k % NCH
+            s0 = stream(bb, c * JC)
+            g = g_of[k]
+            second_add(nc.vector, g, s0, G_J, JC - G_J)
             codes = qpool.tile([P, JC * P], U32, align_bytes=64)
             scl = qpool.tile([P, JC * P], U8, align_bytes=64)
             nc.vector.quantize_mx(
@@ -187,49 +169,44 @@ def tile_graphconvlayer_t_kernel(tc, X, W_gcn, b, H, Wd, out):
             )
             osb = opool.tile([P, JC, F_OUT], F32)
             for h in range(JC // 4):
+                py = psy.tile([P, 4 * P], F32)
+                nc.tensor.matmul_mx(
+                    out=py[:],
+                    lhsT=wc[:].bitcast(FP8X4),
+                    lhsT_scale=ws[:],
+                    rhs=codes[:, h * 4 * P : (h + 1) * 4 * P].bitcast(FP8X4),
+                    rhs_scale=scl[:, h * 4 * P : (h + 1) * 4 * P],
+                    start=True,
+                    stop=True,
+                )
+                ysb = ypool.tile([P, 4 * P], F32)
+                nc.scalar.copy(out=ysb[:], in_=py[:])
                 po = pso.tile([P, 4, F_OUT], F32)
                 for a in range(4):
-                    jl = h * 4 + a
-                    nc.tensor.matmul_mx(
+                    nc.tensor.matmul(
+                        out=po[:, a, :], lhsT=bias_t[:], rhs=ident[:], is_transpose=True, start=True, stop=False
+                    )
+                    nc.tensor.matmul(
                         out=po[:, a, :],
-                        lhsT=codes[:, jl * P : (jl + 1) * P].bitcast(FP8X4),
-                        lhsT_scale=scl[:, jl * P : (jl + 1) * P],
-                        rhs=wc[:].bitcast(FP8X4),
-                        rhs_scale=ws[:],
-                        start=True,
+                        lhsT=ysb[:, a * P : (a + 1) * P],
+                        rhs=ident[:],
+                        is_transpose=True,
+                        start=False,
                         stop=True,
                     )
-                nc.vector.tensor_tensor(out=osb[:, h * 4 : (h + 1) * 4, :], in0=po[:], in1=bias4[:], op=ADD)
+                nc.scalar.copy(out=osb[:, h * 4 : (h + 1) * 4, :], in_=po[:])
             nc.sync.dma_start(
                 out=outv[bb, :, c * JC * F_OUT : (c + 1) * JC * F_OUT],
                 in_=osb[:].rearrange("p j o -> p (j o)"),
             )
 
-        n_chunks = NB * NCH
-        for k in range(n_chunks):
-            bb, c = k // NCH, k % NCH
-            if k + 1 < n_chunks:
-                emit_load_cast(k + 1)
-            s0 = stream(bb, c * JC)
-            if c == 0:
-                emit_pairsum(s0 - 1)
-            first_odd = s0 + (1 - s0 % 2)
-            for off, n in pieces(first_odd // 2, JC // 2):
-                r = (first_odd // 2 + off) % NSO
-                lo = first_odd + 1 + 2 * off
-                nc.scalar.copy(out=dsb[:, r : r + n, 0:4], in_=edge[0][:, lo : lo + 2 * n - 1 : 2, :])
-            g = gpool.tile([P, JC, F_IN], BF16, align_bytes=64)
-            for jl in range(JC):
-                emit_pairsum(s0 + jl)
-                emit_second_add(s0 + jl, g, jl)
-            for off, n in pieces(first_odd // 2, JC // 2):
-                r = (first_odd // 2 + off) % NSO
-                lo = first_odd - 1 + 2 * off
-                j0 = first_odd - s0 + 2 * off
-                nc.vector.tensor_tensor(
-                    out=g[:, j0 : j0 + 2 * n - 1 : 2, 508:512],
-                    in0=dsb[:, r : r + n, 508:512],
-                    in1=edge[1][:, lo : lo + 2 * n - 1 : 2, :],
-                    op=ADD,
-                )
-            emit_back(k, g)
+        n_banks = NB * NCH * 4
+        emit_front(0)
+        for m in range(n_banks):
+            if m + 1 < n_banks:
+                emit_front(m + 1)
+            emit_pairsums(m)
+            if 2 * (m % 4) < G_J:
+                emit_gpsimd_share(m // 4, 2 * (m % 4))
+            if m % 4 == 3:
+                emit_back(m // 4)

@@ -59,8 +59,8 @@ def tile_graphconvlayer_t_kernel(tc, X, W_gcn, b, H, Wd, out):
         make_identity(nc, ident[:])
 
         xtw = const.tile([P, NS * XI * 2], F32)
-        nc.vector.memset(xtw[:], 0.0)
         xtw4 = xtw[:].rearrange("p (s i u) -> p s i u", i=XI, u=2)
+        nc.vector.memset(xtw4[:, :, GH : GH + 4, :], 0.0)
         xtb = xtw[:].bitcast(BF16).rearrange("p (s c) -> p s c", c=XS)
         dr = const.tile([P, NS * DS], F32)
         dv = dr[:].rearrange("p (s c) -> p s c", c=DS)
@@ -82,10 +82,9 @@ def tile_graphconvlayer_t_kernel(tc, X, W_gcn, b, H, Wd, out):
         nc.vector.tensor_tensor(out=bdiag[:], in0=braw[:], in1=ident[:], op=mybir.AluOpType.mult)
         bcol = const.tile([P, 1], F32)
         nc.vector.tensor_reduce(out=bcol[:], in_=bdiag[:], axis=mybir.AxisListType.X, op=ADD)
-        bias_t = const.tile([P, P], F32)
-        nc.vector.tensor_scalar(
-            out=bias_t[:], in0=ident[:], scalar1=0.0, scalar2=bcol[:, 0:1], op0=mybir.AluOpType.mult, op1=ADD
-        )
+        bias4 = const.tile([P, 4, F_OUT], F32)
+        for a in range(4):
+            nc.vector.tensor_copy(out=bias4[:, a, :], in_=braw[:])
 
         xin_of = {}
         bank_of = {}
@@ -104,14 +103,15 @@ def tile_graphconvlayer_t_kernel(tc, X, W_gcn, b, H, Wd, out):
             xw = xin_of[m // 4][:].bitcast(F32)
             bank = pst.tile([P, 4, P], F32)
             for q in range(4):
-                col = (pair * 4 + q) * P
+                u, jl = q // 2, q % 2
+                col = ((pair * 2 + jl) * 2 + u) * P
                 nc.tensor.transpose(out=bank[:, q, :], in_=xw[:, col : col + P], identity=ident[:])
             s0 = stream(bb, c * JC + 2 * pair)
             for off, n in pieces([s0], 2):
                 r = (s0 + off) % NS
                 nc.scalar.copy(
                     out=xtw4[:, r : r + n, 1 : 1 + GH, :],
-                    in_=bank[:, 2 * off : 2 * (off + n), :].rearrange("p (j u) i -> p j i u", u=2),
+                    in_=bank[:].rearrange("p (u j) i -> p j i u", u=2)[:, off : off + n],
                 )
             bank_of[m] = bank
 
@@ -125,17 +125,15 @@ def tile_graphconvlayer_t_kernel(tc, X, W_gcn, b, H, Wd, out):
                 r = (s0 - 1) % NS
                 nc.vector.tensor_copy(out=dv[:, r : r + 1, 4:520], in_=xtb[:, s0 % NS : s0 % NS + 1, 4:520])
             bankb = bank_of[m][:].rearrange("p q i -> p (q i)").bitcast(BF16)
+            bankv = bankb.rearrange("p (u j i e) -> p j i u e", u=2, j=2, e=2)
             for off, n in pieces([s0, s0 + 1], 2):
                 r = (s0 + off) % NS
                 r1 = (s0 + off + 1) % NS
                 nc.scalar.copy(out=dv[:, r : r + n, 4:8], in_=xtb[:, r1 : r1 + n, 4:8])
-            for jl in range(2):
-                r = (s0 + jl) % NS
-                r1 = (s0 + jl + 1) % NS
                 nc.vector.tensor_tensor(
-                    out=dv[:, r, 8:520].rearrange("p (i u e) -> p i u e", u=2, e=2),
-                    in0=bankb[:, jl * 4 * P : (jl + 1) * 4 * P].rearrange("p (u i e) -> p i u e", u=2, e=2),
-                    in1=xtb[:, r1, 8:520].rearrange("p (i u e) -> p i u e", u=2, e=2),
+                    out=dv[:, r : r + n, 8:520].rearrange("p j (i u e) -> p j i u e", u=2, e=2),
+                    in0=bankv[:, off : off + n],
+                    in1=xtb[:, r1 : r1 + n, 8:520].rearrange("p j (i u e) -> p j i u e", u=2, e=2),
                     op=ADD,
                 )
 
@@ -161,44 +159,65 @@ def tile_graphconvlayer_t_kernel(tc, X, W_gcn, b, H, Wd, out):
             bb, c = k // NCH, k % NCH
             s0 = stream(bb, c * JC)
             g = g_of[k]
-            second_add(nc.vector, g, s0, G_J, JC - G_J)
+            last = k == NB * NCH - 1
             codes = qpool.tile([P, JC * P], U32, align_bytes=64)
             scl = qpool.tile([P, JC * P], U8, align_bytes=64)
-            nc.vector.quantize_mx(
-                out=codes[:].bitcast(FP8X4), scales=scl[:], in_=g[:].rearrange("p j c -> p (j c)")
-            )
             osb = opool.tile([P, JC, F_OUT], F32)
-            for h in range(JC // 4):
-                py = psy.tile([P, 4 * P], F32)
-                nc.tensor.matmul_mx(
-                    out=py[:],
-                    lhsT=wc[:].bitcast(FP8X4),
-                    lhsT_scale=ws[:],
-                    rhs=codes[:, h * 4 * P : (h + 1) * 4 * P].bitcast(FP8X4),
-                    rhs_scale=scl[:, h * 4 * P : (h + 1) * 4 * P],
-                    start=True,
-                    stop=True,
+            n_q = 2 if last else 1
+            w = JC // n_q
+            for qi in range(n_q):
+                lo = max(G_J, qi * w)
+                second_add(nc.vector, g, s0, lo, (qi + 1) * w - lo)
+                nc.vector.quantize_mx(
+                    out=codes[:, qi * w * P : (qi + 1) * w * P].bitcast(FP8X4),
+                    scales=scl[:, qi * w * P : (qi + 1) * w * P],
+                    in_=g[:, qi * w : (qi + 1) * w, :].rearrange("p j c -> p (j c)"),
                 )
-                ysb = ypool.tile([P, 4 * P], F32)
-                nc.scalar.copy(out=ysb[:], in_=py[:])
+            for h in range(JC // 4):
+                cols = slice(h * 4 * P, (h + 1) * 4 * P)
                 po = pso.tile([P, 4, F_OUT], F32)
-                for a in range(4):
-                    nc.tensor.matmul(
-                        out=po[:, a, :], lhsT=bias_t[:], rhs=ident[:], is_transpose=True, start=True, stop=False
-                    )
-                    nc.tensor.matmul(
-                        out=po[:, a, :],
-                        lhsT=ysb[:, a * P : (a + 1) * P],
-                        rhs=ident[:],
-                        is_transpose=True,
-                        start=False,
+                if last and h == 1:
+                    for a in range(4):
+                        jl = h * 4 + a
+                        nc.tensor.matmul_mx(
+                            out=po[:, a, :],
+                            lhsT=codes[:, jl * P : (jl + 1) * P].bitcast(FP8X4),
+                            lhsT_scale=scl[:, jl * P : (jl + 1) * P],
+                            rhs=wc[:].bitcast(FP8X4),
+                            rhs_scale=ws[:],
+                            start=True,
+                            stop=True,
+                        )
+                    nc.vector.tensor_tensor(out=osb[:, h * 4 : (h + 1) * 4, :], in0=po[:], in1=bias4[:], op=ADD)
+                else:
+                    py = psy.tile([P, 4 * P], F32)
+                    nc.tensor.matmul_mx(
+                        out=py[:],
+                        lhsT=wc[:].bitcast(FP8X4),
+                        lhsT_scale=ws[:],
+                        rhs=codes[:, cols].bitcast(FP8X4),
+                        rhs_scale=scl[:, cols],
+                        start=True,
                         stop=True,
                     )
-                nc.scalar.copy(out=osb[:, h * 4 : (h + 1) * 4, :], in_=po[:])
-            nc.sync.dma_start(
-                out=outv[bb, :, c * JC * F_OUT : (c + 1) * JC * F_OUT],
-                in_=osb[:].rearrange("p j o -> p (j o)"),
-            )
+                    ysb = ypool.tile([P, 4 * P], F32)
+                    nc.scalar.activation(
+                        out=ysb[:], in_=py[:], func=mybir.ActivationFunctionType.Identity, bias=bcol[:, 0:1], scale=1.0
+                    )
+                    for a in range(4):
+                        nc.tensor.transpose(out=po[:, a, :], in_=ysb[:, a * P : (a + 1) * P], identity=ident[:])
+                    nc.scalar.copy(out=osb[:, h * 4 : (h + 1) * 4, :], in_=po[:])
+                if last:
+                    lo = (c * JC + h * 4) * F_OUT
+                    nc.sync.dma_start(
+                        out=outv[bb, :, lo : lo + 4 * F_OUT],
+                        in_=osb[:, h * 4 : (h + 1) * 4, :].rearrange("p j o -> p (j o)"),
+                    )
+            if not last:
+                nc.sync.dma_start(
+                    out=outv[bb, :, c * JC * F_OUT : (c + 1) * JC * F_OUT],
+                    in_=osb[:].rearrange("p j o -> p (j o)"),
+                )
 
         n_banks = NB * NCH * 4
         emit_front(0)

@@ -148,12 +148,15 @@ def tile_graphconvlayer_t_kernel(tc, X, W_gcn, b, H, Wd, out):
                     op=ADD,
                 )
 
-        def emit_gpsimd_share(k, lo):
+        def emit_gpsimd_share(k):
             bb, c = k // NCH, k % NCH
-            if lo == 0:
-                g = gpool.tile([P, JC, F_IN], BF16, align_bytes=64)
-                g_of[k] = g
-            second_add(nc.gpsimd, g_of[k], stream(bb, c * JC), lo, min(2, G_J - lo))
+            g = gpool.tile([P, JC, F_IN], BF16, align_bytes=64)
+            g_of[k] = g
+            second_add(nc.gpsimd, g, stream(bb, c * JC), 0, G_J)
+
+        def emit_vector_share(k, lo, cnt):
+            bb, c = k // NCH, k % NCH
+            second_add(nc.vector, g_of[k], stream(bb, c * JC), lo, cnt)
 
         def emit_back(k):
             bb, c = k // NCH, k % NCH
@@ -166,8 +169,6 @@ def tile_graphconvlayer_t_kernel(tc, X, W_gcn, b, H, Wd, out):
             n_q = 2 if last else 1
             w = JC // n_q
             for qi in range(n_q):
-                lo = max(G_J, qi * w)
-                second_add(nc.vector, g, s0, lo, (qi + 1) * w - lo)
                 nc.vector.quantize_mx(
                     out=codes[:, qi * w * P : (qi + 1) * w * P].bitcast(FP8X4),
                     scales=scl[:, qi * w * P : (qi + 1) * w * P],
@@ -225,7 +226,11 @@ def tile_graphconvlayer_t_kernel(tc, X, W_gcn, b, H, Wd, out):
             if m + 1 < n_banks:
                 emit_front(m + 1)
             emit_pairsums(m)
-            if 2 * (m % 4) < G_J:
-                emit_gpsimd_share(m // 4, 2 * (m % 4))
+            k = m // 4
+            if m % 4 == 1:
+                emit_gpsimd_share(k)
             if m % 4 == 3:
-                emit_back(m // 4)
+                emit_vector_share(k, G_J, JC - G_J)
+                if k > 0:
+                    emit_back(k - 1)
+        emit_back(NB * NCH - 1)

@@ -20,7 +20,7 @@ NS = 24
 XI = 132
 XS = XI * 4
 DS = 520
-G_J = 3
+G_J = 4
 
 
 def pieces(starts, n):
@@ -47,13 +47,16 @@ def tile_graphconvlayer_t_kernel(tc, X, W_gcn, b, H, Wd, out):
     with ExitStack() as ctx:
         const = ctx.enter_context(tc.tile_pool(name="const", bufs=1))
         xpool = ctx.enter_context(tc.tile_pool(name="xin", bufs=4))
-        gpool = ctx.enter_context(tc.tile_pool(name="grouped", bufs=3))
+        ggpool = ctx.enter_context(tc.tile_pool(name="grouped_g", bufs=1))
+        gvpool = ctx.enter_context(tc.tile_pool(name="grouped_v", bufs=2))
         qpool = ctx.enter_context(tc.tile_pool(name="quant", bufs=2))
         opool = ctx.enter_context(tc.tile_pool(name="outsb", bufs=3))
         pst = ctx.enter_context(tc.psum_pool(name="pst", bufs=4))
         psy = ctx.enter_context(tc.psum_pool(name="psy", bufs=2))
         pso = ctx.enter_context(tc.psum_pool(name="pso", bufs=2))
         ypool = ctx.enter_context(tc.tile_pool(name="ysb", bufs=3))
+
+        ctx.enter_context(tc.manual_schedule())
 
         ident = const.tile([P, P], F32)
         make_identity(nc, ident[:])
@@ -67,39 +70,47 @@ def tile_graphconvlayer_t_kernel(tc, X, W_gcn, b, H, Wd, out):
 
         wraw = const.tile([P, 2, 2 * F_OUT], BF16)
         nc.scalar.dma_start(out=wraw[:], in_=W_gcn.rearrange("(u p e) c -> p u (e c)", u=2, e=2))
-        wg = const.tile([P, 4 * F_OUT], BF16, align_bytes=64)
-        nc.vector.tensor_copy(
-            out=wg[:].rearrange("p (c u e) -> p c u e", u=2, e=2),
-            in_=wraw[:].rearrange("p u (e c) -> p c u e", e=2),
-        )
-        wc = const.tile([P, F_OUT], U32, align_bytes=64)
-        ws = const.tile([P, F_OUT], U8, align_bytes=64)
-        nc.vector.quantize_mx(out=wc[:].bitcast(FP8X4), scales=ws[:], in_=wg[:])
-
         braw = const.tile([P, F_OUT], BF16)
         nc.scalar.dma_start(out=braw[:], in_=b.partition_broadcast(P))
+        wg = const.tile([P, 4 * F_OUT], BF16, align_bytes=64)
+        wc = const.tile([P, F_OUT], U32, align_bytes=64)
+        ws = const.tile([P, F_OUT], U8, align_bytes=64)
         bdiag = const.tile([P, F_OUT], F32)
-        nc.vector.tensor_tensor(out=bdiag[:], in0=braw[:], in1=ident[:], op=mybir.AluOpType.mult)
         bcol = const.tile([P, 1], F32)
-        nc.vector.tensor_reduce(out=bcol[:], in_=bdiag[:], axis=mybir.AxisListType.X, op=ADD)
         bias4 = const.tile([P, 4, F_OUT], F32)
-        for a in range(4):
-            nc.vector.tensor_copy(out=bias4[:, a, :], in_=braw[:])
 
+        def emit_constants():
+            nc.vector.tensor_copy(
+                out=wg[:].rearrange("p (c u e) -> p c u e", u=2, e=2),
+                in_=wraw[:].rearrange("p u (e c) -> p c u e", e=2),
+            )
+            nc.vector.tensor_tensor(out=bdiag[:], in0=braw[:], in1=ident[:], op=mybir.AluOpType.mult)
+            nc.vector.quantize_mx(out=wc[:].bitcast(FP8X4), scales=ws[:], in_=wg[:])
+            nc.vector.tensor_reduce(out=bcol[:], in_=bdiag[:], axis=mybir.AxisListType.X, op=ADD)
+            for a in range(4):
+                nc.vector.tensor_copy(out=bias4[:, a, :], in_=braw[:])
+
+        n_chunks = NB * NCH
         xin_of = {}
         bank_of = {}
-        g_of = {}
+        gg_of = {}
+        gv_of = {}
+        q_of = {}
+        y_of = {}
+        o_of = {}
+
+        def emit_load(k):
+            bb, c = k // NCH, k % NCH
+            xin = xpool.tile([P, JC * F_IN], BF16)
+            n_dma = 4 if k == 0 else 1
+            w = JC * F_IN // n_dma
+            for d in range(n_dma):
+                lo = c * JC * F_IN + d * w
+                nc.sync.dma_start(out=xin[:, d * w : (d + 1) * w], in_=xv[bb, :, lo : lo + w])
+            xin_of[k] = xin
 
         def emit_front(m):
             bb, c, pair = m // (4 * NCH), (m // 4) % NCH, m % 4
-            if pair == 0:
-                xin = xpool.tile([P, JC * F_IN], BF16)
-                n_dma = 4 if m == 0 else 1
-                w = JC * F_IN // n_dma
-                for d in range(n_dma):
-                    lo = c * JC * F_IN + d * w
-                    nc.sync.dma_start(out=xin[:, d * w : (d + 1) * w], in_=xv[bb, :, lo : lo + w])
-                xin_of[m // 4] = xin
             xw = xin_of[m // 4][:].bitcast(F32)
             bank = pst.tile([P, 4, P], F32)
             for q in range(4):
@@ -115,21 +126,32 @@ def tile_graphconvlayer_t_kernel(tc, X, W_gcn, b, H, Wd, out):
                 )
             bank_of[m] = bank
 
+        def emit_edges(k):
+            bb, c = k // NCH, k % NCH
+            s0 = stream(bb, c * JC)
+            if c == 0:
+                r = (s0 - 1) % NS
+                nc.vector.tensor_copy(out=dv[:, r : r + 1, 4:520], in_=xtb[:, s0 % NS : s0 % NS + 1, 4:520])
+            if c == NCH - 1:
+                z = (s0 + JC) % NS
+                nc.vector.memset(xtw4[:, z : z + 1, :, :], 0.0)
+
+        def emit_fill(m):
+            bb, c, pair = m // (4 * NCH), (m // 4) % NCH, m % 4
+            s0 = stream(bb, c * JC + 2 * pair)
+            for off, n in pieces([s0, s0 + 1], 2):
+                r = (s0 + off) % NS
+                r1 = (s0 + off + 1) % NS
+                nc.scalar.copy(out=dv[:, r : r + n, 4:8], in_=xtb[:, r1 : r1 + n, 4:8])
+
         def emit_pairsums(m):
             bb, c, pair = m // (4 * NCH), (m // 4) % NCH, m % 4
             s0 = stream(bb, c * JC + 2 * pair)
-            if c == NCH - 1 and pair == 3:
-                z = (s0 + 2) % NS
-                nc.vector.memset(xtw4[:, z : z + 1, :, :], 0.0)
-            if c == 0 and pair == 0:
-                r = (s0 - 1) % NS
-                nc.vector.tensor_copy(out=dv[:, r : r + 1, 4:520], in_=xtb[:, s0 % NS : s0 % NS + 1, 4:520])
             bankb = bank_of[m][:].rearrange("p q i -> p (q i)").bitcast(BF16)
             bankv = bankb.rearrange("p (u j i e) -> p j i u e", u=2, j=2, e=2)
             for off, n in pieces([s0, s0 + 1], 2):
                 r = (s0 + off) % NS
                 r1 = (s0 + off + 1) % NS
-                nc.scalar.copy(out=dv[:, r : r + n, 4:8], in_=xtb[:, r1 : r1 + n, 4:8])
                 nc.vector.tensor_tensor(
                     out=dv[:, r : r + n, 8:520].rearrange("p j (i u e) -> p j i u e", u=2, e=2),
                     in0=bankv[:, off : off + n],
@@ -137,100 +159,146 @@ def tile_graphconvlayer_t_kernel(tc, X, W_gcn, b, H, Wd, out):
                     op=ADD,
                 )
 
-        def second_add(eng, g, s0, lo, cnt):
+        def second_add(eng, g, k, lo, cnt):
+            s0 = stream(k // NCH, (k % NCH) * JC)
             for off, n in pieces([s0 + lo, s0 + lo - 1], cnt):
                 r = (s0 + lo + off) % NS
                 rm = (s0 + lo + off - 1) % NS
                 eng.tensor_tensor(
-                    out=g[:, lo + off : lo + off + n, :],
+                    out=g[:, (lo + off) % 4 : (lo + off) % 4 + n, :],
                     in0=dv[:, r : r + n, 4:516],
                     in1=dv[:, rm : rm + n, 8:520],
                     op=ADD,
                 )
 
-        def emit_gpsimd_share(k):
-            bb, c = k // NCH, k % NCH
-            g = gpool.tile([P, JC, F_IN], BF16, align_bytes=64)
-            g_of[k] = g
-            second_add(nc.gpsimd, g, stream(bb, c * JC), 0, G_J)
+        def emit_low_half(k, eng, cnt):
+            gg = ggpool.tile([P, 4, F_IN], BF16, align_bytes=64)
+            gg_of[k] = gg
+            if k == 0:
+                nc.vector.memset(gg[:, 0, 0:16], 0.0)
+            second_add(eng, gg, k, 0, cnt)
 
-        def emit_vector_share(k, lo, cnt):
-            bb, c = k // NCH, k % NCH
-            second_add(nc.vector, g_of[k], stream(bb, c * JC), lo, cnt)
+        def emit_high_half(k):
+            gv = gvpool.tile([P, 4, F_IN], BF16, align_bytes=64)
+            gv_of[k] = gv
+            second_add(nc.vector, gv, k, 4, 4)
 
-        def emit_back(k):
-            bb, c = k // NCH, k % NCH
-            s0 = stream(bb, c * JC)
-            g = g_of[k]
-            last = k == NB * NCH - 1
-            codes = qpool.tile([P, JC * P], U32, align_bytes=64)
-            scl = qpool.tile([P, JC * P], U8, align_bytes=64)
-            osb = opool.tile([P, JC, F_OUT], F32)
-            n_q = 2 if last else 1
-            w = JC // n_q
-            for qi in range(n_q):
-                nc.vector.quantize_mx(
-                    out=codes[:, qi * w * P : (qi + 1) * w * P].bitcast(FP8X4),
-                    scales=scl[:, qi * w * P : (qi + 1) * w * P],
-                    in_=g[:, qi * w : (qi + 1) * w, :].rearrange("p j c -> p (j c)"),
+        def emit_quant(k, h):
+            if k not in q_of:
+                codes = qpool.tile([P, JC * P], U32, align_bytes=64)
+                scl = qpool.tile([P, JC * P], U8, align_bytes=64)
+                q_of[k] = (codes, scl)
+            codes, scl = q_of[k]
+            g = gg_of[k] if h == 0 else gv_of[k]
+            cols = slice(h * 4 * P, (h + 1) * 4 * P)
+            nc.vector.quantize_mx(
+                out=codes[:, cols].bitcast(FP8X4), scales=scl[:, cols], in_=g[:].rearrange("p j c -> p (j c)")
+            )
+
+        def emit_product(k, h):
+            codes, scl = q_of[k]
+            cols = slice(h * 4 * P, (h + 1) * 4 * P)
+            py = psy.tile([P, 4 * P], F32)
+            nc.tensor.matmul_mx(
+                out=py[:],
+                lhsT=wc[:].bitcast(FP8X4),
+                lhsT_scale=ws[:],
+                rhs=codes[:, cols].bitcast(FP8X4),
+                rhs_scale=scl[:, cols],
+                start=True,
+                stop=True,
+            )
+            ysb = ypool.tile([P, 4 * P], F32)
+            nc.scalar.activation(
+                out=ysb[:], in_=py[:], func=mybir.ActivationFunctionType.Identity, bias=bcol[:, 0:1], scale=1.0
+            )
+            y_of[(k, h)] = ysb
+
+        def out_tile(k):
+            if k not in o_of:
+                osb = opool.tile([P, JC, F_OUT], F32)
+                o_of[k] = osb
+            return o_of[k]
+
+        def emit_turn_back(k, h):
+            ysb = y_of[(k, h)]
+            po = pso.tile([P, 4, F_OUT], F32)
+            for a in range(4):
+                nc.tensor.transpose(out=po[:, a, :], in_=ysb[:, a * P : (a + 1) * P], identity=ident[:])
+            nc.scalar.copy(out=out_tile(k)[:, h * 4 : (h + 1) * 4, :], in_=po[:])
+
+        def emit_direct(k, h):
+            codes, scl = q_of[k]
+            po = pso.tile([P, 4, F_OUT], F32)
+            for a in range(4):
+                jl = h * 4 + a
+                nc.tensor.matmul_mx(
+                    out=po[:, a, :],
+                    lhsT=codes[:, jl * P : (jl + 1) * P].bitcast(FP8X4),
+                    lhsT_scale=scl[:, jl * P : (jl + 1) * P],
+                    rhs=wc[:].bitcast(FP8X4),
+                    rhs_scale=ws[:],
+                    start=True,
+                    stop=True,
                 )
-            for h in range(JC // 4):
-                cols = slice(h * 4 * P, (h + 1) * 4 * P)
-                po = pso.tile([P, 4, F_OUT], F32)
-                if last and h == 1:
-                    for a in range(4):
-                        jl = h * 4 + a
-                        nc.tensor.matmul_mx(
-                            out=po[:, a, :],
-                            lhsT=codes[:, jl * P : (jl + 1) * P].bitcast(FP8X4),
-                            lhsT_scale=scl[:, jl * P : (jl + 1) * P],
-                            rhs=wc[:].bitcast(FP8X4),
-                            rhs_scale=ws[:],
-                            start=True,
-                            stop=True,
-                        )
-                    nc.vector.tensor_tensor(out=osb[:, h * 4 : (h + 1) * 4, :], in0=po[:], in1=bias4[:], op=ADD)
-                else:
-                    py = psy.tile([P, 4 * P], F32)
-                    nc.tensor.matmul_mx(
-                        out=py[:],
-                        lhsT=wc[:].bitcast(FP8X4),
-                        lhsT_scale=ws[:],
-                        rhs=codes[:, cols].bitcast(FP8X4),
-                        rhs_scale=scl[:, cols],
-                        start=True,
-                        stop=True,
-                    )
-                    ysb = ypool.tile([P, 4 * P], F32)
-                    nc.scalar.activation(
-                        out=ysb[:], in_=py[:], func=mybir.ActivationFunctionType.Identity, bias=bcol[:, 0:1], scale=1.0
-                    )
-                    for a in range(4):
-                        nc.tensor.transpose(out=po[:, a, :], in_=ysb[:, a * P : (a + 1) * P], identity=ident[:])
-                    nc.scalar.copy(out=osb[:, h * 4 : (h + 1) * 4, :], in_=po[:])
-                if last:
-                    lo = (c * JC + h * 4) * F_OUT
-                    nc.sync.dma_start(
-                        out=outv[bb, :, lo : lo + 4 * F_OUT],
-                        in_=osb[:, h * 4 : (h + 1) * 4, :].rearrange("p j o -> p (j o)"),
-                    )
-            if not last:
-                nc.sync.dma_start(
-                    out=outv[bb, :, c * JC * F_OUT : (c + 1) * JC * F_OUT],
-                    in_=osb[:].rearrange("p j o -> p (j o)"),
-                )
+            nc.vector.tensor_tensor(out=out_tile(k)[:, h * 4 : (h + 1) * 4, :], in0=po[:], in1=bias4[:], op=ADD)
 
-        n_banks = NB * NCH * 4
-        emit_front(0)
-        for m in range(n_banks):
-            if m + 1 < n_banks:
-                emit_front(m + 1)
-            emit_pairsums(m)
-            k = m // 4
-            if m % 4 == 1:
-                emit_gpsimd_share(k)
-            if m % 4 == 3:
-                emit_vector_share(k, G_J, JC - G_J)
-                if k > 0:
-                    emit_back(k - 1)
-        emit_back(NB * NCH - 1)
+        def emit_store(k, lo, cnt):
+            bb, c = k // NCH, k % NCH
+            a = (c * JC + lo) * F_OUT
+            nc.sync.dma_start(
+                out=outv[bb, :, a : a + cnt * F_OUT],
+                in_=out_tile(k)[:, lo : lo + cnt, :].rearrange("p j o -> p (j o)"),
+            )
+
+        for k in range(3):
+            emit_load(k)
+        emit_constants()
+        for m in range(4):
+            emit_front(m)
+        emit_edges(0)
+        for m in range(3):
+            emit_fill(m)
+        last = n_chunks - 1
+        for k in range(n_chunks):
+            emit_pairsums(4 * k)
+            if k >= 2:
+                emit_product(k - 2, 0)
+                emit_product(k - 2, 1)
+            if k < last:
+                emit_front(4 * (k + 1))
+            emit_fill(4 * k + 3)
+            emit_pairsums(4 * k + 1)
+            if k >= 2:
+                emit_turn_back(k - 2, 0)
+                emit_turn_back(k - 2, 1)
+                emit_store(k - 2, 0, JC)
+            emit_pairsums(4 * k + 2)
+            emit_pairsums(4 * k + 3)
+            emit_high_half(k)
+            if k < last:
+                emit_edges(k + 1)
+            if k >= 1:
+                emit_quant(k - 1, 1)
+                emit_quant(k - 1, 0)
+            if k < last:
+                emit_low_half(k, nc.gpsimd, G_J)
+                for pair in range(1, 4):
+                    emit_front(4 * (k + 1) + pair)
+                for pair in range(3):
+                    emit_fill(4 * (k + 1) + pair)
+            if k + 3 < n_chunks:
+                emit_load(k + 3)
+        emit_quant(last, 1)
+        emit_low_half(last, nc.vector, 4)
+        emit_quant(last, 0)
+        for h in range(2):
+            emit_product(last - 1, h)
+        emit_product(last, 1)
+        for h in range(2):
+            emit_turn_back(last - 1, h)
+        emit_store(last - 1, 0, JC)
+        emit_turn_back(last, 1)
+        emit_store(last, 4, 4)
+        emit_direct(last, 0)
+        emit_store(last, 0, 4)

from contextlib import ExitStack

import concourse.mybir as mybir
from concourse.masks import make_identity

F32 = mybir.dt.float32
BF16 = mybir.dt.bfloat16
U32 = mybir.dt.uint32
U8 = mybir.dt.uint8
FP8X4 = mybir.dt.float8_e4m3fn_x4
ADD = mybir.AluOpType.add

P = 128
NB, GH, GW, F_IN, F_OUT = 2, 128, 64, 512, 128
FLOPS = 2 * NB * GH * GW * F_IN * F_OUT

JC = 8
NCH = GW // JC
NS = 24
XI = 132
XS = XI * 4
DS = 520
G_J = 4


def pieces(starts, n):
    cuts = [0, n]
    for st in starts:
        k = NS - st % NS
        while k < n:
            cuts.append(k)
            k += NS
    cs = sorted(set(cuts))
    return [(cs[i], cs[i + 1] - cs[i]) for i in range(len(cs) - 1)]


def stream(bb, j):
    return 1 + bb * (GW + 1) + j


def tile_graphconvlayer_t_kernel(tc, X, W_gcn, b, H, Wd, out):
    nc = tc.nc
    assert H == GH and Wd == GW
    xv = X.rearrange("b (i j) f -> b i (j f)", j=GW)
    outv = out.rearrange("b (i j) o -> b i (j o)", j=GW)

    with ExitStack() as ctx:
        const = ctx.enter_context(tc.tile_pool(name="const", bufs=1))
        xpool = ctx.enter_context(tc.tile_pool(name="xin", bufs=4))
        ggpool = ctx.enter_context(tc.tile_pool(name="grouped_g", bufs=1))
        gvpool = ctx.enter_context(tc.tile_pool(name="grouped_v", bufs=2))
        qpool = ctx.enter_context(tc.tile_pool(name="quant", bufs=2))
        opool = ctx.enter_context(tc.tile_pool(name="outsb", bufs=3))
        pst = ctx.enter_context(tc.psum_pool(name="pst", bufs=4))
        psy = ctx.enter_context(tc.psum_pool(name="psy", bufs=2))
        pso = ctx.enter_context(tc.psum_pool(name="pso", bufs=2))
        ypool = ctx.enter_context(tc.tile_pool(name="ysb", bufs=3))

        ctx.enter_context(tc.manual_schedule())

        ident = const.tile([P, P], F32)
        make_identity(nc, ident[:])

        xtw = const.tile([P, NS * XI * 2], F32)
        xtw4 = xtw[:].rearrange("p (s i u) -> p s i u", i=XI, u=2)
        nc.vector.memset(xtw4[:, :, GH : GH + 4, :], 0.0)
        xtb = xtw[:].bitcast(BF16).rearrange("p (s c) -> p s c", c=XS)
        dr = const.tile([P, NS * DS], F32)
        dv = dr[:].rearrange("p (s c) -> p s c", c=DS)

        wraw = const.tile([P, 2, 2 * F_OUT], BF16)
        nc.scalar.dma_start(out=wraw[:], in_=W_gcn.rearrange("(u p e) c -> p u (e c)", u=2, e=2))
        braw = const.tile([P, F_OUT], BF16)
        nc.scalar.dma_start(out=braw[:], in_=b.partition_broadcast(P))
        wg = const.tile([P, 4 * F_OUT], BF16, align_bytes=64)
        wc = const.tile([P, F_OUT], U32, align_bytes=64)
        ws = const.tile([P, F_OUT], U8, align_bytes=64)
        bdiag = const.tile([P, F_OUT], F32)
        bcol = const.tile([P, 1], F32)
        bias4 = const.tile([P, 4, F_OUT], F32)

        def emit_constants():
            nc.vector.tensor_copy(
                out=wg[:].rearrange("p (c u e) -> p c u e", u=2, e=2),
                in_=wraw[:].rearrange("p u (e c) -> p c u e", e=2),
            )
            nc.vector.tensor_tensor(out=bdiag[:], in0=braw[:], in1=ident[:], op=mybir.AluOpType.mult)
            nc.vector.quantize_mx(out=wc[:].bitcast(FP8X4), scales=ws[:], in_=wg[:])
            nc.vector.tensor_reduce(out=bcol[:], in_=bdiag[:], axis=mybir.AxisListType.X, op=ADD)
            for a in range(4):
                nc.vector.tensor_copy(out=bias4[:, a, :], in_=braw[:])

        n_chunks = NB * NCH
        xin_of = {}
        bank_of = {}
        gg_of = {}
        gv_of = {}
        q_of = {}
        y_of = {}
        o_of = {}

        def emit_load(k):
            bb, c = k // NCH, k % NCH
            xin = xpool.tile([P, JC * F_IN], BF16)
            n_dma = 4 if k == 0 else 1
            w = JC * F_IN // n_dma
            for d in range(n_dma):
                lo = c * JC * F_IN + d * w
                nc.sync.dma_start(out=xin[:, d * w : (d + 1) * w], in_=xv[bb, :, lo : lo + w])
            xin_of[k] = xin

        def emit_front(m):
            bb, c, pair = m // (4 * NCH), (m // 4) % NCH, m % 4
            xw = xin_of[m // 4][:].bitcast(F32)
            bank = pst.tile([P, 4, P], F32)
            for q in range(4):
                u, jl = q // 2, q % 2
                col = ((pair * 2 + jl) * 2 + u) * P
                nc.tensor.transpose(out=bank[:, q, :], in_=xw[:, col : col + P], identity=ident[:])
            s0 = stream(bb, c * JC + 2 * pair)
            for off, n in pieces([s0], 2):
                r = (s0 + off) % NS
                nc.scalar.copy(
                    out=xtw4[:, r : r + n, 1 : 1 + GH, :],
                    in_=bank[:].rearrange("p (u j) i -> p j i u", u=2)[:, off : off + n],
                )
            bank_of[m] = bank

        def emit_edges(k):
            bb, c = k // NCH, k % NCH
            s0 = stream(bb, c * JC)
            if c == 0:
                r = (s0 - 1) % NS
                nc.vector.tensor_copy(out=dv[:, r : r + 1, 4:520], in_=xtb[:, s0 % NS : s0 % NS + 1, 4:520])
            if c == NCH - 1:
                z = (s0 + JC) % NS
                nc.vector.memset(xtw4[:, z : z + 1, :, :], 0.0)

        def emit_fill(m):
            bb, c, pair = m // (4 * NCH), (m // 4) % NCH, m % 4
            s0 = stream(bb, c * JC + 2 * pair)
            for off, n in pieces([s0, s0 + 1], 2):
                r = (s0 + off) % NS
                r1 = (s0 + off + 1) % NS
                nc.scalar.copy(out=dv[:, r : r + n, 4:8], in_=xtb[:, r1 : r1 + n, 4:8])

        def emit_pairsums(m):
            bb, c, pair = m // (4 * NCH), (m // 4) % NCH, m % 4
            s0 = stream(bb, c * JC + 2 * pair)
            bankb = bank_of[m][:].rearrange("p q i -> p (q i)").bitcast(BF16)
            bankv = bankb.rearrange("p (u j i e) -> p j i u e", u=2, j=2, e=2)
            for off, n in pieces([s0, s0 + 1], 2):
                r = (s0 + off) % NS
                r1 = (s0 + off + 1) % NS
                nc.vector.tensor_tensor(
                    out=dv[:, r : r + n, 8:520].rearrange("p j (i u e) -> p j i u e", u=2, e=2),
                    in0=bankv[:, off : off + n],
                    in1=xtb[:, r1 : r1 + n, 8:520].rearrange("p j (i u e) -> p j i u e", u=2, e=2),
                    op=ADD,
                )

        def second_add(eng, g, k, lo, cnt):
            s0 = stream(k // NCH, (k % NCH) * JC)
            for off, n in pieces([s0 + lo, s0 + lo - 1], cnt):
                r = (s0 + lo + off) % NS
                rm = (s0 + lo + off - 1) % NS
                eng.tensor_tensor(
                    out=g[:, (lo + off) % 4 : (lo + off) % 4 + n, :],
                    in0=dv[:, r : r + n, 4:516],
                    in1=dv[:, rm : rm + n, 8:520],
                    op=ADD,
                )

        def emit_low_half(k, eng, cnt):
            gg = ggpool.tile([P, 4, F_IN], BF16, align_bytes=64)
            gg_of[k] = gg
            if k == 0:
                nc.vector.memset(gg[:, 0, 0:16], 0.0)
            second_add(eng, gg, k, 0, cnt)

        def emit_high_half(k):
            gv = gvpool.tile([P, 4, F_IN], BF16, align_bytes=64)
            gv_of[k] = gv
            second_add(nc.vector, gv, k, 4, 4)

        def emit_quant(k, h):
            if k not in q_of:
                codes = qpool.tile([P, JC * P], U32, align_bytes=64)
                scl = qpool.tile([P, JC * P], U8, align_bytes=64)
                q_of[k] = (codes, scl)
            codes, scl = q_of[k]
            g = gg_of[k] if h == 0 else gv_of[k]
            cols = slice(h * 4 * P, (h + 1) * 4 * P)
            nc.vector.quantize_mx(
                out=codes[:, cols].bitcast(FP8X4), scales=scl[:, cols], in_=g[:].rearrange("p j c -> p (j c)")
            )

        def emit_product(k, h):
            codes, scl = q_of[k]
            cols = slice(h * 4 * P, (h + 1) * 4 * P)
            py = psy.tile([P, 4 * P], F32)
            nc.tensor.matmul_mx(
                out=py[:],
                lhsT=wc[:].bitcast(FP8X4),
                lhsT_scale=ws[:],
                rhs=codes[:, cols].bitcast(FP8X4),
                rhs_scale=scl[:, cols],
                start=True,
                stop=True,
            )
            ysb = ypool.tile([P, 4 * P], F32)
            nc.scalar.activation(
                out=ysb[:], in_=py[:], func=mybir.ActivationFunctionType.Identity, bias=bcol[:, 0:1], scale=1.0
            )
            y_of[(k, h)] = ysb

        def out_tile(k):
            if k not in o_of:
                osb = opool.tile([P, JC, F_OUT], F32)
                o_of[k] = osb
            return o_of[k]

        def emit_turn_back(k, h):
            ysb = y_of[(k, h)]
            po = pso.tile([P, 4, F_OUT], F32)
            for a in range(4):
                nc.tensor.transpose(out=po[:, a, :], in_=ysb[:, a * P : (a + 1) * P], identity=ident[:])
            nc.scalar.copy(out=out_tile(k)[:, h * 4 : (h + 1) * 4, :], in_=po[:])

        def emit_direct(k, h):
            codes, scl = q_of[k]
            po = pso.tile([P, 4, F_OUT], F32)
            for a in range(4):
                jl = h * 4 + a
                nc.tensor.matmul_mx(
                    out=po[:, a, :],
                    lhsT=codes[:, jl * P : (jl + 1) * P].bitcast(FP8X4),
                    lhsT_scale=scl[:, jl * P : (jl + 1) * P],
                    rhs=wc[:].bitcast(FP8X4),
                    rhs_scale=ws[:],
                    start=True,
                    stop=True,
                )
            nc.vector.tensor_tensor(out=out_tile(k)[:, h * 4 : (h + 1) * 4, :], in0=po[:], in1=bias4[:], op=ADD)

        def emit_store(k, lo, cnt):
            bb, c = k // NCH, k % NCH
            a = (c * JC + lo) * F_OUT
            nc.sync.dma_start(
                out=outv[bb, :, a : a + cnt * F_OUT],
                in_=out_tile(k)[:, lo : lo + cnt, :].rearrange("p j o -> p (j o)"),
            )

        for k in range(3):
            emit_load(k)
        emit_constants()
        for m in range(4):
            emit_front(m)
        emit_edges(0)
        for m in range(3):
            emit_fill(m)
        last = n_chunks - 1
        for k in range(n_chunks):
            emit_pairsums(4 * k)
            if k >= 2:
                emit_product(k - 2, 0)
                emit_product(k - 2, 1)
            if k < last:
                emit_front(4 * (k + 1))
            emit_fill(4 * k + 3)
            emit_pairsums(4 * k + 1)
            if k >= 2:
                emit_turn_back(k - 2, 0)
                emit_turn_back(k - 2, 1)
                emit_store(k - 2, 0, JC)
            emit_pairsums(4 * k + 2)
            emit_pairsums(4 * k + 3)
            emit_high_half(k)
            if k < last:
                emit_edges(k + 1)
            if k >= 1:
                emit_quant(k - 1, 1)
                emit_quant(k - 1, 0)
            if k < last:
                emit_low_half(k, nc.gpsimd, G_J)
                for pair in range(1, 4):
                    emit_front(4 * (k + 1) + pair)
                for pair in range(3):
                    emit_fill(4 * (k + 1) + pair)
            if k + 3 < n_chunks:
                emit_load(k + 3)
        emit_quant(last, 1)
        emit_low_half(last, nc.vector, 4)
        emit_quant(last, 0)
        for h in range(2):
            emit_product(last - 1, h)
        emit_product(last, 1)
        for h in range(2):
            emit_turn_back(last - 1, h)
        emit_store(last - 1, 0, JC)
        emit_turn_back(last, 1)
        emit_store(last, 4, 4)
        emit_direct(last, 0)
        emit_store(last, 0, 4)
